import numpy as np
import ml_dtypes


def mxq(x, axis, fmt="e4m3"):
    dtype, down = {"e4m3": (ml_dtypes.float8_e4m3fn, 7), "e5m2": (ml_dtypes.float8_e5m2, 14)}[fmt]
    v = np.moveaxis(np.asarray(x, np.float32).astype(ml_dtypes.bfloat16).astype(np.float64), axis, -1)
    blocks = v.reshape(v.shape[:-1] + (-1, 32))
    amax = np.abs(blocks).max(-1, keepdims=True)
    byte = np.maximum(np.where(amax > 0, np.frexp(amax)[1] - 1 + 127, 0) - down, 1)
    scale = np.exp2(byte - 127.0)
    codes = (blocks / scale).astype(np.float32).astype(dtype).astype(np.float64)
    return np.moveaxis((codes * scale).reshape(v.shape), -1, axis)


WIDE = False


def mx_kscale(k):
    if not WIDE:
        return np.ones(k)
    levels = np.array([20, -20, 10, -10, 0])
    a = np.random.permutation(np.resize(levels, k // 512 * 4)).reshape(k // 512, 4)
    idx = np.arange(k)
    return np.exp2(a[idx // 512, idx % 128 // 32])


BF16 = ml_dtypes.bfloat16


def bf(x):
    return np.asarray(x, np.float32).astype(BF16)


def f64(x):
    return np.asarray(x).astype(np.float64)


P = 16
B, C, IH, IW = 16, 4, 256, 256
D = 1024
DIN = C * P * P
GH, GW = IH // P, IW // P
NP = GH * GW
SEQ = NP + 1


def _patchify(x):
    nb, nc_, h, w = x.shape
    gh, gw = h // P, w // P
    x = x.reshape(nb, nc_, gh, P, gw, P)
    x = x.transpose(0, 2, 4, 1, 3, 5)
    return x.reshape(nb, gh * gw, nc_ * P * P)


def _unpatchify(p, nc_, gh, gw):
    nb = p.shape[0]
    p = p.reshape(nb, gh, gw, nc_, P, P)
    p = p.transpose(0, 3, 1, 4, 2, 5)
    return p.reshape(nb, nc_, gh * P, gw * P)


def setup_inputs():
    u = mx_kscale(D)
    x = np.random.standard_normal((B, C, IH, IW))
    W = np.random.standard_normal((D, DIN)) * 0.03 / u[:, None]
    b = np.random.standard_normal(D) * 0.1
    class_token = np.random.standard_normal(D)
    pos_emb = np.random.standard_normal((SEQ, D))
    g = np.random.standard_normal((B, SEQ, D)) * np.exp2(np.random.randint(-12, 1, (B, SEQ, 1))) * 4.0 * u[None, None, :]
    return {"x": bf(x), "W": bf(W), "b": bf(b), "class_token": bf(class_token),
            "pos_emb": bf(pos_emb), "grad_out": bf(g)}


def reference(x, W, b, class_token, pos_emb, grad_out):
    g = f64(grad_out)[:, 1:, :].reshape(B * NP, D)
    gp = mxq(g, 1, "e5m2") @ mxq(f64(W), 0, "e4m3")
    return _unpatchify(gp.reshape(B, NP, DIN), C, GH, GW)

@@ -1,0 +1,150 @@
+from contextlib import ExitStack
+
+import concourse.mybir as mybir
+from concourse.masks import make_identity
+
+F32 = mybir.dt.float32
+BF16 = mybir.dt.bfloat16
+U32 = mybir.dt.uint32
+U8 = mybir.dt.uint8
+E4M3X4 = mybir.dt.float8_e4m3fn_x4
+E5M2X4 = mybir.dt.float8_e5m2_x4
+
+P = 128
+FLOPS = 2 * 4096 * 1024 * 1024
+BYTES = 4096 * 1024 * 2 + 1024 * 1024 * 2 + 4096 * 1024 * 4
+
+
+def tile_patchpositionembedding_kernel(tc, x, W, b, class_token, pos_emb, grad_out, out):
+    nc = tc.nc
+    with ExitStack() as ctx:
+        keep = ctx.enter_context(tc.tile_pool(name="keep", bufs=1))
+        big = ctx.enter_context(tc.tile_pool(name="big", bufs=4))
+        stg = ctx.enter_context(tc.tile_pool(name="stg", bufs=3))
+        wst = ctx.enter_context(tc.tile_pool(name="wst", bufs=2))
+        pst = ctx.enter_context(tc.psum_pool(name="pst", bufs=4))
+        psa = ctx.enter_context(tc.psum_pool(name="psa", bufs=4))
+
+        ident = keep.tile([P, P], F32, name="ident")
+        make_identity(nc, ident[:])
+
+        wraw = keep.tile([P, 8, 1024], BF16, name="wraw")
+        wcodes = keep.tile([P, 2, 1024], U32, name="wcodes", align_bytes=64)
+        wscales = keep.tile([P, 2, 1024], U8, name="wscales", align_bytes=64)
+        gcodes = [keep.tile([P, 4096], U32, name="gcodes%d" % h, align_bytes=64) for h in range(2)]
+        gscales = [keep.tile([P, 4096], U8, name="gscales%d" % h, align_bytes=64) for h in range(2)]
+        graw = [big.tile([P, 16 * 1024], BF16, name="graw%d" % h, tag="big") for h in range(2)]
+
+        def load_g(h, w0, w1):
+            src = grad_out[:, 1 + 128 * h : 1 + 128 * (h + 1), :].rearrange("b (g w) k -> b g w k", g=8)
+            nc.sync.dma_start(
+                out=graw[h][:, w0 * 1024 : w1 * 1024],
+                in_=src[:, :, w0:w1, :].rearrange("b g w k -> b g (w k)"),
+            )
+
+        def load_w(g):
+            src = W[512 * g : 512 * (g + 1), :].rearrange("(u q e) n -> q u (e n)", u=2, q=128, e=2)
+            nc.sync.dma_start(
+                out=wraw[:, 4 * g : 4 * g + 4, :].rearrange("p (u e) n -> p u (e n)", e=2),
+                in_=src,
+            )
+
+        load_g(0, 0, 2)
+        load_w(0)
+        load_w(1)
+        load_g(0, 2, 4)
+        for j in range(1, 4):
+            load_g(0, 4 * j, 4 * j + 4)
+        for j in range(4):
+            load_g(1, 4 * j, 4 * j + 4)
+
+        def prep_w(n):
+            for g in range(2):
+                wg = wst.tile([P, 512, 4], BF16, name="wg", tag="wg", align_bytes=64)
+                nc.vector.tensor_copy(
+                    out=wg[:].rearrange("p (c i) t -> p c t i", i=4),
+                    in_=wraw[:, 4 * g : 4 * g + 4, 512 * n : 512 * (n + 1)].rearrange("p t (c i) -> p c t i", i=4),
+                )
+                nc.vector.quantize_mx(
+                    out=wcodes[:, g, 512 * n : 512 * (n + 1)].bitcast(E4M3X4),
+                    scales=wscales[:, g, 512 * n : 512 * (n + 1)],
+                    in_=wg[:].rearrange("p c t -> p (c t)"),
+                )
+
+        def flip(h, j):
+            words = graw[h][:].bitcast(F32)
+            stage = stg.tile([P, 4096], BF16, name="stage", tag="stage", align_bytes=64)
+            s32 = stage[:].bitcast(F32)
+            for i in range(4):
+                gw = 4 * j + i
+                xt = pst.tile([P, 4, P], F32, name="xt", tag="xt")
+                for a in range(4):
+                    nc.tensor.transpose(xt[:, a, :], words[:, 512 * gw + 128 * a : 512 * gw + 128 * (a + 1)], ident[:])
+                nc.scalar.copy(
+                    out=s32[:, 512 * i : 512 * (i + 1)].rearrange("p (g r u) -> p g r u", g=2, r=128, u=2),
+                    in_=xt[:].rearrange("p (g u) r -> p g r u", g=2, u=2),
+                )
+            nc.vector.quantize_mx(
+                out=gcodes[h][:, 1024 * j : 1024 * (j + 1)].bitcast(E5M2X4),
+                scales=gscales[h][:, 1024 * j : 1024 * (j + 1)],
+                in_=stage[:],
+            )
+
+        otiles = {}
+
+        def mult(h, n, j):
+            if j == 0:
+                otiles[(h, n)] = big.tile([P, 2, 16, 16, 16], F32, name="o%d%d" % (h, n), tag="big")
+            o = otiles[(h, n)]
+            for i in range(4):
+                gw = 4 * j + i
+                acc = psa.tile([P, 512], F32, name="acc", tag="acc")
+                for g in range(2):
+                    cols = slice(128 * (2 * gw + g), 128 * (2 * gw + g + 1))
+                    nc.tensor.matmul_mx(
+                        out=acc[:],
+                        lhsT=gcodes[h][:, cols].bitcast(E5M2X4),
+                        lhsT_scale=gscales[h][:, cols],
+                        rhs=wcodes[:, g, 512 * n : 512 * (n + 1)].bitcast(E4M3X4),
+                        rhs_scale=wscales[:, g, 512 * n : 512 * (n + 1)],
+                        start=(g == 0),
+                        stop=(g == 1),
+                    )
+                src = acc[:].rearrange("p (c r w) -> p c r w", c=2, r=16, w=16)
+                if i % 2 == 0:
+                    nc.vector.tensor_copy(out=o[:, :, :, gw, :], in_=src)
+                else:
+                    nc.scalar.copy(out=o[:, :, :, gw, :], in_=src)
+
+        def store(h, n):
+            o = otiles[(h, n)]
+            for c in range(2):
+                nc.sync.dma_start(
+                    out=out[:, 2 * n + c, 128 * h : 128 * (h + 1), :].rearrange("b (g r) x -> b g (r x)", g=8),
+                    in_=o[:, c].rearrange("p r w x -> p (r w x)"),
+                )
+
+        flip(0, 0)
+        prep_w(0)
+        flip(0, 1)
+        mult(0, 0, 0)
+        flip(0, 2)
+        mult(0, 0, 1)
+        flip(0, 3)
+        mult(0, 0, 2)
+        prep_w(1)
+        flip(1, 0)
+        mult(0, 0, 3)
+        store(0, 0)
+        mult(0, 1, 0)
+        flip(1, 1)
+        mult(0, 1, 1)
+        flip(1, 2)
+        mult(0, 1, 2)
+        flip(1, 3)
+        mult(0, 1, 3)
+        store(0, 1)
+        for n in range(2):
+            for j in range(4):
+                mult(1, n, j)
+            store(1, n)

@@ -27,8 +27,9 @@ def tile_patchpositionembedding_kernel(tc, x, W, b, class_token, pos_emb, grad_o
 
         ident = keep.tile([P, P], F32, name="ident")
         make_identity(nc, ident[:])
+        ctx.enter_context(tc.manual_schedule())
 
-        wraw = keep.tile([P, 8, 1024], BF16, name="wraw")
+        wraw = [keep.tile([P, 8, 512], BF16, name="wraw%d" % n) for n in range(2)]
         wcodes = keep.tile([P, 2, 1024], U32, name="wcodes", align_bytes=64)
         wscales = keep.tile([P, 2, 1024], U8, name="wscales", align_bytes=64)
         gcodes = [keep.tile([P, 4096], U32, name="gcodes%d" % h, align_bytes=64) for h in range(2)]
@@ -42,52 +43,64 @@ def tile_patchpositionembedding_kernel(tc, x, W, b, class_token, pos_emb, grad_o
                 in_=src[:, :, w0:w1, :].rearrange("b g w k -> b g (w k)"),
             )
 
-        def load_w(g):
-            src = W[512 * g : 512 * (g + 1), :].rearrange("(u q e) n -> q u (e n)", u=2, q=128, e=2)
-            nc.sync.dma_start(
-                out=wraw[:, 4 * g : 4 * g + 4, :].rearrange("p (u e) n -> p u (e n)", e=2),
-                in_=src,
-            )
+        def load_w(n):
+            for a in range(4):
+                nc.sync.dma_start(
+                    out=wraw[n][:, 2 * a : 2 * a + 2, :],
+                    in_=W[256 * a : 256 * (a + 1), 512 * n : 512 * (n + 1)].rearrange("(q e) c -> q e c", e=2),
+                )
 
         load_g(0, 0, 2)
         load_w(0)
-        load_w(1)
         load_g(0, 2, 4)
         for j in range(1, 4):
             load_g(0, 4 * j, 4 * j + 4)
         for j in range(4):
             load_g(1, 4 * j, 4 * j + 4)
+        load_w(1)
 
-        def prep_w(n):
-            for g in range(2):
-                wg = wst.tile([P, 512, 4], BF16, name="wg", tag="wg", align_bytes=64)
-                nc.vector.tensor_copy(
-                    out=wg[:].rearrange("p (c i) t -> p c t i", i=4),
-                    in_=wraw[:, 4 * g : 4 * g + 4, 512 * n : 512 * (n + 1)].rearrange("p t (c i) -> p c t i", i=4),
-                )
-                nc.vector.quantize_mx(
-                    out=wcodes[:, g, 512 * n : 512 * (n + 1)].bitcast(E4M3X4),
-                    scales=wscales[:, g, 512 * n : 512 * (n + 1)],
-                    in_=wg[:].rearrange("p c t -> p (c t)"),
-                )
+        wgs = {}
 
-        def flip(h, j):
+        def regroup_w(n, g):
+            wg = wst.tile([P, 512, 4], BF16, name="wg", tag="wg", align_bytes=64)
+            wgs[(n, g)] = wg
+            nc.vector.tensor_copy(
+                out=wg[:].rearrange("p (c i) t -> p c t i", i=4),
+                in_=wraw[n][:, 4 * g : 4 * g + 4, :].rearrange("p t (c i) -> p c t i", i=4),
+            )
+
+        def quant_w(n, g):
+            nc.vector.quantize_mx(
+                out=wcodes[:, g, 512 * n : 512 * (n + 1)].bitcast(E4M3X4),
+                scales=wscales[:, g, 512 * n : 512 * (n + 1)],
+                in_=wgs[(n, g)][:].rearrange("p c t -> p (c t)"),
+            )
+
+        stages = {}
+
+        def flip(h, j, i0, i1):
             words = graw[h][:].bitcast(F32)
-            stage = stg.tile([P, 4096], BF16, name="stage", tag="stage", align_bytes=64)
-            s32 = stage[:].bitcast(F32)
-            for i in range(4):
+            if i0 == 0:
+                stages[(h, j)] = stg.tile([P, 4096], BF16, name="stage", tag="stage", align_bytes=64)
+            s32 = stages[(h, j)][:].bitcast(F32)
+            for i in range(i0, i1):
                 gw = 4 * j + i
                 xt = pst.tile([P, 4, P], F32, name="xt", tag="xt")
                 for a in range(4):
                     nc.tensor.transpose(xt[:, a, :], words[:, 512 * gw + 128 * a : 512 * gw + 128 * (a + 1)], ident[:])
-                nc.scalar.copy(
-                    out=s32[:, 512 * i : 512 * (i + 1)].rearrange("p (g r u) -> p g r u", g=2, r=128, u=2),
-                    in_=xt[:].rearrange("p (g u) r -> p g r u", g=2, u=2),
-                )
+                dst = s32[:, 512 * i : 512 * (i + 1)].rearrange("p (g r u) -> p g r u", g=2, r=128, u=2)
+                src = xt[:].rearrange("p (g u) r -> p g r u", g=2, u=2)
+                if i == 0:
+                    nc.scalar.copy(out=dst, in_=src)
+                else:
+                    nc.vector.tensor_copy(out=dst, in_=src)
+
+        def quant_g(h, j, i0, i1):
+            cols = slice(1024 * j + 256 * i0, 1024 * j + 256 * i1)
             nc.vector.quantize_mx(
-                out=gcodes[h][:, 1024 * j : 1024 * (j + 1)].bitcast(E5M2X4),
-                scales=gscales[h][:, 1024 * j : 1024 * (j + 1)],
-                in_=stage[:],
+                out=gcodes[h][:, cols].bitcast(E5M2X4),
+                scales=gscales[h][:, cols],
+                in_=stages[(h, j)][:, 1024 * i0 : 1024 * i1],
             )
 
         otiles = {}
@@ -111,40 +124,31 @@ def tile_patchpositionembedding_kernel(tc, x, W, b, class_token, pos_emb, grad_o
                         stop=(g == 1),
                     )
                 src = acc[:].rearrange("p (c r w) -> p c r w", c=2, r=16, w=16)
-                if i % 2 == 0:
-                    nc.vector.tensor_copy(out=o[:, :, :, gw, :], in_=src)
-                else:
-                    nc.scalar.copy(out=o[:, :, :, gw, :], in_=src)
+                nc.scalar.copy(out=o[:, :, :, gw, :], in_=src)
+            if j == 3:
+                for c in range(2):
+                    nc.sync.dma_start(
+                        out=out[:, 2 * n + c, 128 * h : 128 * (h + 1), :].rearrange("b (g r) x -> b g (r x)", g=8),
+                        in_=o[:, c].rearrange("p r w x -> p (r w x)"),
+                    )
 
-        def store(h, n):
-            o = otiles[(h, n)]
-            for c in range(2):
-                nc.sync.dma_start(
-                    out=out[:, 2 * n + c, 128 * h : 128 * (h + 1), :].rearrange("b (g r) x -> b g (r x)", g=8),
-                    in_=o[:, c].rearrange("p r w x -> p (r w x)"),
-                )
-
-        flip(0, 0)
-        prep_w(0)
-        flip(0, 1)
-        mult(0, 0, 0)
-        flip(0, 2)
-        mult(0, 0, 1)
-        flip(0, 3)
-        mult(0, 0, 2)
-        prep_w(1)
-        flip(1, 0)
-        mult(0, 0, 3)
-        store(0, 0)
-        mult(0, 1, 0)
-        flip(1, 1)
-        mult(0, 1, 1)
-        flip(1, 2)
-        mult(0, 1, 2)
-        flip(1, 3)
-        mult(0, 1, 3)
-        store(0, 1)
-        for n in range(2):
-            for j in range(4):
-                mult(1, n, j)
-            store(1, n)
+        flip(0, 0, 0, 2)
+        regroup_w(0, 0)
+        quant_g(0, 0, 0, 2)
+        regroup_w(0, 1)
+        quant_w(0, 0)
+        quant_w(0, 1)
+        flip(0, 0, 2, 4)
+        quant_g(0, 0, 2, 4)
+        quads = [(h, j) for h in range(2) for j in range(4)]
+        late_w = [lambda: regroup_w(1, 0), lambda: quant_w(1, 0), lambda: regroup_w(1, 1), lambda: quant_w(1, 1)]
+        for t in range(8):
+            if t + 1 < 8:
+                h, j = quads[t + 1]
+                flip(h, j, 0, 4)
+                quant_g(h, j, 0, 4)
+            if t >= 4:
+                late_w[t - 4]()
+            mult(quads[t][0], 0, quads[t][1])
+        for h, j in quads:
+            mult(h, 1, j)

@@ -64,10 +64,12 @@ def tile_patchpositionembedding_kernel(tc, x, W, b, class_token, pos_emb, grad_o
         def regroup_w(n, g):
             wg = wst.tile([P, 512, 4], BF16, name="wg", tag="wg", align_bytes=64)
             wgs[(n, g)] = wg
-            nc.vector.tensor_copy(
-                out=wg[:].rearrange("p (c i) t -> p c t i", i=4),
-                in_=wraw[n][:, 4 * g : 4 * g + 4, :].rearrange("p t (c i) -> p c t i", i=4),
-            )
+            dst = wg[:].rearrange("p (c i) t -> p c t i", i=4)
+            src = wraw[n][:, 4 * g : 4 * g + 4, :].rearrange("p t (c i) -> p c t i", i=4)
+            if n == 0:
+                nc.vector.tensor_copy(out=dst, in_=src)
+            else:
+                nc.scalar.copy(out=dst, in_=src)
 
         def quant_w(n, g):
             nc.vector.quantize_mx(
@@ -90,10 +92,7 @@ def tile_patchpositionembedding_kernel(tc, x, W, b, class_token, pos_emb, grad_o
                     nc.tensor.transpose(xt[:, a, :], words[:, 512 * gw + 128 * a : 512 * gw + 128 * (a + 1)], ident[:])
                 dst = s32[:, 512 * i : 512 * (i + 1)].rearrange("p (g r u) -> p g r u", g=2, r=128, u=2)
                 src = xt[:].rearrange("p (g u) r -> p g r u", g=2, u=2)
-                if i == 0:
-                    nc.scalar.copy(out=dst, in_=src)
-                else:
-                    nc.vector.tensor_copy(out=dst, in_=src)
+                nc.scalar.copy(out=dst, in_=src)
 
         def quant_g(h, j, i0, i1):
             cols = slice(1024 * j + 256 * i0, 1024 * j + 256 * i1)
@@ -105,7 +104,7 @@ def tile_patchpositionembedding_kernel(tc, x, W, b, class_token, pos_emb, grad_o
 
         otiles = {}
 
-        def mult(h, n, j):
+        def mult(h, n, j, after_first=None):
             if j == 0:
                 otiles[(h, n)] = big.tile([P, 2, 16, 16, 16], F32, name="o%d%d" % (h, n), tag="big")
             o = otiles[(h, n)]
@@ -124,7 +123,9 @@ def tile_patchpositionembedding_kernel(tc, x, W, b, class_token, pos_emb, grad_o
                         stop=(g == 1),
                     )
                 src = acc[:].rearrange("p (c r w) -> p c r w", c=2, r=16, w=16)
-                nc.scalar.copy(out=o[:, :, :, gw, :], in_=src)
+                nc.vector.tensor_copy(out=o[:, :, :, gw, :], in_=src)
+                if i == 0 and after_first is not None:
+                    after_first()
             if j == 3:
                 for c in range(2):
                     nc.sync.dma_start(
@@ -143,12 +144,13 @@ def tile_patchpositionembedding_kernel(tc, x, W, b, class_token, pos_emb, grad_o
         quads = [(h, j) for h in range(2) for j in range(4)]
         late_w = [lambda: regroup_w(1, 0), lambda: quant_w(1, 0), lambda: regroup_w(1, 1), lambda: quant_w(1, 1)]
         for t in range(8):
+            hook = None
             if t + 1 < 8:
                 h, j = quads[t + 1]
                 flip(h, j, 0, 4)
-                quant_g(h, j, 0, 4)
+                hook = lambda h=h, j=j: quant_g(h, j, 0, 4)
             if t >= 4:
                 late_w[t - 4]()
-            mult(quads[t][0], 0, quads[t][1])
+            mult(quads[t][0], 0, quads[t][1], hook)
         for h, j in quads:
             mult(h, 1, j)

@@ -124,6 +124,7 @@ def tile_patchpositionembedding_kernel(tc, x, W, b, class_token, pos_emb, grad_o
                     )
                 src = acc[:].rearrange("p (c r w) -> p c r w", c=2, r=16, w=16)
                 nc.vector.tensor_copy(out=o[:, :, :, gw, :], in_=src)
+                nc.vector.tensor_copy(out=o[:, :, :, gw, :], in_=src)
                 if i == 0 and after_first is not None:
                     after_first()
             if j == 3:

@@ -19,11 +19,11 @@ def tile_patchpositionembedding_kernel(tc, x, W, b, class_token, pos_emb, grad_o
     nc = tc.nc
     with ExitStack() as ctx:
         keep = ctx.enter_context(tc.tile_pool(name="keep", bufs=1))
-        big = ctx.enter_context(tc.tile_pool(name="big", bufs=4))
-        stg = ctx.enter_context(tc.tile_pool(name="stg", bufs=3))
-        wst = ctx.enter_context(tc.tile_pool(name="wst", bufs=2))
-        pst = ctx.enter_context(tc.psum_pool(name="pst", bufs=4))
-        psa = ctx.enter_context(tc.psum_pool(name="psa", bufs=4))
+        big = ctx.enter_context(tc.tile_pool(name="big", bufs=1))
+        stg = ctx.enter_context(tc.tile_pool(name="stg", bufs=1))
+        wst = ctx.enter_context(tc.tile_pool(name="wst", bufs=1))
+        pst = ctx.enter_context(tc.psum_pool(name="pst", bufs=1))
+        psa = ctx.enter_context(tc.psum_pool(name="psa", bufs=1))
 
         ident = keep.tile([P, P], F32, name="ident")
         make_identity(nc, ident[:])
@@ -34,7 +34,7 @@ def tile_patchpositionembedding_kernel(tc, x, W, b, class_token, pos_emb, grad_o
         wscales = keep.tile([P, 2, 1024], U8, name="wscales", align_bytes=64)
         gcodes = [keep.tile([P, 4096], U32, name="gcodes%d" % h, align_bytes=64) for h in range(2)]
         gscales = [keep.tile([P, 4096], U8, name="gscales%d" % h, align_bytes=64) for h in range(2)]
-        graw = [big.tile([P, 16 * 1024], BF16, name="graw%d" % h, tag="big") for h in range(2)]
+        graw = [big.tile([P, 16 * 1024], BF16, name="graw%d" % h, tag="big%d" % h) for h in range(2)]
 
         def load_g(h, w0, w1):
             src = grad_out[:, 1 + 128 * h : 1 + 128 * (h + 1), :].rearrange("b (g w) k -> b g w k", g=8)
@@ -62,14 +62,12 @@ def tile_patchpositionembedding_kernel(tc, x, W, b, class_token, pos_emb, grad_o
         wgs = {}
 
         def regroup_w(n, g):
-            wg = wst.tile([P, 512, 4], BF16, name="wg", tag="wg", align_bytes=64)
+            wg = wst.tile([P, 512, 4], BF16, name="wg%d%d" % (n, g), tag="wg%d" % g, align_bytes=64)
             wgs[(n, g)] = wg
-            dst = wg[:].rearrange("p (c i) t -> p c t i", i=4)
-            src = wraw[n][:, 4 * g : 4 * g + 4, :].rearrange("p t (c i) -> p c t i", i=4)
-            if n == 0:
-                nc.vector.tensor_copy(out=dst, in_=src)
-            else:
-                nc.scalar.copy(out=dst, in_=src)
+            nc.vector.tensor_copy(
+                out=wg[:].rearrange("p (c i) t -> p c t i", i=4),
+                in_=wraw[n][:, 4 * g : 4 * g + 4, :].rearrange("p t (c i) -> p c t i", i=4),
+            )
 
         def quant_w(n, g):
             nc.vector.quantize_mx(
@@ -83,16 +81,19 @@ def tile_patchpositionembedding_kernel(tc, x, W, b, class_token, pos_emb, grad_o
         def flip(h, j, i0, i1):
             words = graw[h][:].bitcast(F32)
             if i0 == 0:
-                stages[(h, j)] = stg.tile([P, 4096], BF16, name="stage", tag="stage", align_bytes=64)
+                stages[(h, j)] = stg.tile([P, 4096], BF16, name="stage%d%d" % (h, j), tag="stage%d" % ((4 * h + j) % 3), align_bytes=64)
             s32 = stages[(h, j)][:].bitcast(F32)
             for i in range(i0, i1):
                 gw = 4 * j + i
-                xt = pst.tile([P, 4, P], F32, name="xt", tag="xt")
+                xt = pst.tile([P, 4, P], F32, name="xt%d_%d" % (h, gw), tag="xt%d" % i)
                 for a in range(4):
                     nc.tensor.transpose(xt[:, a, :], words[:, 512 * gw + 128 * a : 512 * gw + 128 * (a + 1)], ident[:])
                 dst = s32[:, 512 * i : 512 * (i + 1)].rearrange("p (g r u) -> p g r u", g=2, r=128, u=2)
                 src = xt[:].rearrange("p (g u) r -> p g r u", g=2, u=2)
-                nc.scalar.copy(out=dst, in_=src)
+                if i == 0:
+                    nc.scalar.copy(out=dst, in_=src)
+                else:
+                    nc.vector.tensor_copy(out=dst, in_=src)
 
         def quant_g(h, j, i0, i1):
             cols = slice(1024 * j + 256 * i0, 1024 * j + 256 * i1)
@@ -104,13 +105,13 @@ def tile_patchpositionembedding_kernel(tc, x, W, b, class_token, pos_emb, grad_o
 
         otiles = {}
 
-        def mult(h, n, j, after_first=None):
+        def mult(h, n, j):
             if j == 0:
-                otiles[(h, n)] = big.tile([P, 2, 16, 16, 16], F32, name="o%d%d" % (h, n), tag="big")
+                otiles[(h, n)] = big.tile([P, 2, 16, 16, 16], F32, name="o%d%d" % (h, n), tag="big%d" % (h if n == 1 else 2 + h))
             o = otiles[(h, n)]
             for i in range(4):
                 gw = 4 * j + i
-                acc = psa.tile([P, 512], F32, name="acc", tag="acc")
+                acc = psa.tile([P, 512], F32, name="acc%d%d_%d" % (h, n, gw), tag="acc%d" % i)
                 for g in range(2):
                     cols = slice(128 * (2 * gw + g), 128 * (2 * gw + g + 1))
                     nc.tensor.matmul_mx(
@@ -123,10 +124,7 @@ def tile_patchpositionembedding_kernel(tc, x, W, b, class_token, pos_emb, grad_o
                         stop=(g == 1),
                     )
                 src = acc[:].rearrange("p (c r w) -> p c r w", c=2, r=16, w=16)
-                nc.vector.tensor_copy(out=o[:, :, :, gw, :], in_=src)
-                nc.vector.tensor_copy(out=o[:, :, :, gw, :], in_=src)
-                if i == 0 and after_first is not None:
-                    after_first()
+                nc.scalar.copy(out=o[:, :, :, gw, :], in_=src)
             if j == 3:
                 for c in range(2):
                     nc.sync.dma_start(
@@ -145,13 +143,12 @@ def tile_patchpositionembedding_kernel(tc, x, W, b, class_token, pos_emb, grad_o
         quads = [(h, j) for h in range(2) for j in range(4)]
         late_w = [lambda: regroup_w(1, 0), lambda: quant_w(1, 0), lambda: regroup_w(1, 1), lambda: quant_w(1, 1)]
         for t in range(8):
-            hook = None
             if t + 1 < 8:
                 h, j = quads[t + 1]
                 flip(h, j, 0, 4)
-                hook = lambda h=h, j=j: quant_g(h, j, 0, 4)
+                quant_g(h, j, 0, 4)
             if t >= 4:
                 late_w[t - 4]()
-            mult(quads[t][0], 0, quads[t][1], hook)
+            mult(quads[t][0], 0, quads[t][1])
         for h, j in quads:
             mult(h, 1, j)

@@ -22,8 +22,7 @@ def tile_patchpositionembedding_kernel(tc, x, W, b, class_token, pos_emb, grad_o
         big = ctx.enter_context(tc.tile_pool(name="big", bufs=1))
         stg = ctx.enter_context(tc.tile_pool(name="stg", bufs=1))
         wst = ctx.enter_context(tc.tile_pool(name="wst", bufs=1))
-        pst = ctx.enter_context(tc.psum_pool(name="pst", bufs=1))
-        psa = ctx.enter_context(tc.psum_pool(name="psa", bufs=1))
+        psum = ctx.enter_context(tc.psum_pool(name="psum", bufs=1))
 
         ident = keep.tile([P, P], F32, name="ident")
         make_identity(nc, ident[:])
@@ -77,23 +76,39 @@ def tile_patchpositionembedding_kernel(tc, x, W, b, class_token, pos_emb, grad_o
             )
 
         stages = {}
+        otiles = {}
+        order = {}
 
-        def flip(h, j, i0, i1):
+        def batch(key, tags, items, fill, drain):
+            f = order.get(key, tags)
+            n = len(f)
+            tiles = [fill(items[k], f[k]) for k in range(n)]
+            d = [n - 1] + list(range(n - 1))
+            for k in d:
+                drain(items[k], tiles[k])
+            order[key] = [f[d[-1]]] + [f[k] for k in d[:-1]]
+
+        def fill_t(item, tag):
+            h, gw = item
             words = graw[h][:].bitcast(F32)
+            xt = psum.tile([P, 4, P], F32, name="xt%d_%d" % (h, gw), tag=tag)
+            for a in range(4):
+                nc.tensor.transpose(xt[:, a, :], words[:, 512 * gw + 128 * a : 512 * gw + 128 * (a + 1)], ident[:])
+            return xt
+
+        def drain_t(item, xt):
+            h, gw = item
+            i = gw % 4
+            s32 = stages[(h, gw // 4)][:].bitcast(F32)
+            nc.vector.tensor_copy(
+                out=s32[:, 512 * i : 512 * (i + 1)].rearrange("p (g r u) -> p g r u", g=2, r=128, u=2),
+                in_=xt[:].rearrange("p (g u) r -> p g r u", g=2, u=2),
+            )
+
+        def flip(h, j, i0, i1, key, tags):
             if i0 == 0:
                 stages[(h, j)] = stg.tile([P, 4096], BF16, name="stage%d%d" % (h, j), tag="stage%d" % ((4 * h + j) % 3), align_bytes=64)
-            s32 = stages[(h, j)][:].bitcast(F32)
-            for i in range(i0, i1):
-                gw = 4 * j + i
-                xt = pst.tile([P, 4, P], F32, name="xt%d_%d" % (h, gw), tag="xt%d" % i)
-                for a in range(4):
-                    nc.tensor.transpose(xt[:, a, :], words[:, 512 * gw + 128 * a : 512 * gw + 128 * (a + 1)], ident[:])
-                dst = s32[:, 512 * i : 512 * (i + 1)].rearrange("p (g r u) -> p g r u", g=2, r=128, u=2)
-                src = xt[:].rearrange("p (g u) r -> p g r u", g=2, u=2)
-                if i == 0:
-                    nc.scalar.copy(out=dst, in_=src)
-                else:
-                    nc.vector.tensor_copy(out=dst, in_=src)
+            batch(key, tags, [(h, 4 * j + i) for i in range(i0, i1)], fill_t, drain_t)
 
         def quant_g(h, j, i0, i1):
             cols = slice(1024 * j + 256 * i0, 1024 * j + 256 * i1)
@@ -103,52 +118,63 @@ def tile_patchpositionembedding_kernel(tc, x, W, b, class_token, pos_emb, grad_o
                 in_=stages[(h, j)][:, 1024 * i0 : 1024 * i1],
             )
 
-        otiles = {}
+        def fill_x(item, tag):
+            h, n, gw = item
+            acc = psum.tile([P, 512], F32, name="acc%d%d_%d" % (h, n, gw), tag=tag)
+            for g in range(2):
+                cols = slice(128 * (2 * gw + g), 128 * (2 * gw + g + 1))
+                nc.tensor.matmul_mx(
+                    out=acc[:],
+                    lhsT=gcodes[h][:, cols].bitcast(E5M2X4),
+                    lhsT_scale=gscales[h][:, cols],
+                    rhs=wcodes[:, g, 512 * n : 512 * (n + 1)].bitcast(E4M3X4),
+                    rhs_scale=wscales[:, g, 512 * n : 512 * (n + 1)],
+                    start=(g == 0),
+                    stop=(g == 1),
+                )
+            return acc
 
-        def mult(h, n, j):
-            if j == 0:
+        def drain_x(item, acc):
+            h, n, gw = item
+            nc.scalar.copy(
+                out=otiles[(h, n)][:, :, :, gw, :],
+                in_=acc[:].rearrange("p (c r w) -> p c r w", c=2, r=16, w=16),
+            )
+
+        def mult(h, n, w0, w1, key, tags):
+            if w0 == 0:
                 otiles[(h, n)] = big.tile([P, 2, 16, 16, 16], F32, name="o%d%d" % (h, n), tag="big%d" % (h if n == 1 else 2 + h))
-            o = otiles[(h, n)]
-            for i in range(4):
-                gw = 4 * j + i
-                acc = psa.tile([P, 512], F32, name="acc%d%d_%d" % (h, n, gw), tag="acc%d" % i)
-                for g in range(2):
-                    cols = slice(128 * (2 * gw + g), 128 * (2 * gw + g + 1))
-                    nc.tensor.matmul_mx(
-                        out=acc[:],
-                        lhsT=gcodes[h][:, cols].bitcast(E5M2X4),
-                        lhsT_scale=gscales[h][:, cols],
-                        rhs=wcodes[:, g, 512 * n : 512 * (n + 1)].bitcast(E4M3X4),
-                        rhs_scale=wscales[:, g, 512 * n : 512 * (n + 1)],
-                        start=(g == 0),
-                        stop=(g == 1),
-                    )
-                src = acc[:].rearrange("p (c r w) -> p c r w", c=2, r=16, w=16)
-                nc.scalar.copy(out=o[:, :, :, gw, :], in_=src)
-            if j == 3:
+            batch(key, tags, [(h, n, gw) for gw in range(w0, w1)], fill_x, drain_x)
+            if w1 == 16:
                 for c in range(2):
                     nc.sync.dma_start(
                         out=out[:, 2 * n + c, 128 * h : 128 * (h + 1), :].rearrange("b (g r) x -> b g (r x)", g=8),
-                        in_=o[:, c].rearrange("p r w x -> p (r w x)"),
+                        in_=otiles[(h, n)][:, c].rearrange("p r w x -> p (r w x)"),
                     )
 
-        flip(0, 0, 0, 2)
+        LOW = ["pb0", "pb1", "pb2", "pb3"]
+        HIGH = ["pb4", "pb5", "pb6", "pb7"]
+
+        flip(0, 0, 0, 2, "ta", LOW[0:2])
         regroup_w(0, 0)
         quant_g(0, 0, 0, 2)
         regroup_w(0, 1)
         quant_w(0, 0)
         quant_w(0, 1)
-        flip(0, 0, 2, 4)
+        flip(0, 0, 2, 4, "tb", LOW[2:4])
         quant_g(0, 0, 2, 4)
         quads = [(h, j) for h in range(2) for j in range(4)]
         late_w = [lambda: regroup_w(1, 0), lambda: quant_w(1, 0), lambda: regroup_w(1, 1), lambda: quant_w(1, 1)]
         for t in range(8):
             if t + 1 < 8:
                 h, j = quads[t + 1]
-                flip(h, j, 0, 4)
+                flip(h, j, 0, 4, "t", LOW)
                 quant_g(h, j, 0, 4)
             if t >= 4:
                 late_w[t - 4]()
-            mult(quads[t][0], 0, quads[t][1])
-        for h, j in quads:
-            mult(h, 1, j)
+            h, j = quads[t]
+            mult(h, 0, 4 * j, 4 * j + 2, "xa", HIGH[0:2])
+            mult(h, 0, 4 * j + 2, 4 * j + 4, "xb", HIGH[2:4])
+        for t in range(8):
+            h, j = quads[t]
+            mult(h, 1, 4 * j, 4 * j + 4, "m%d" % (t % 2), LOW if t % 2 == 0 else HIGH)

@@ -22,7 +22,8 @@ def tile_patchpositionembedding_kernel(tc, x, W, b, class_token, pos_emb, grad_o
         big = ctx.enter_context(tc.tile_pool(name="big", bufs=1))
         stg = ctx.enter_context(tc.tile_pool(name="stg", bufs=1))
         wst = ctx.enter_context(tc.tile_pool(name="wst", bufs=1))
-        psum = ctx.enter_context(tc.psum_pool(name="psum", bufs=1))
+        pst = ctx.enter_context(tc.psum_pool(name="pst", bufs=1))
+        psa = ctx.enter_context(tc.psum_pool(name="psa", bufs=1))
 
         ident = keep.tile([P, P], F32, name="ident")
         make_identity(nc, ident[:])
@@ -76,39 +77,23 @@ def tile_patchpositionembedding_kernel(tc, x, W, b, class_token, pos_emb, grad_o
             )
 
         stages = {}
-        otiles = {}
-        order = {}
 
-        def batch(key, tags, items, fill, drain):
-            f = order.get(key, tags)
-            n = len(f)
-            tiles = [fill(items[k], f[k]) for k in range(n)]
-            d = [n - 1] + list(range(n - 1))
-            for k in d:
-                drain(items[k], tiles[k])
-            order[key] = [f[d[-1]]] + [f[k] for k in d[:-1]]
-
-        def fill_t(item, tag):
-            h, gw = item
+        def flip(h, j, i0, i1):
             words = graw[h][:].bitcast(F32)
-            xt = psum.tile([P, 4, P], F32, name="xt%d_%d" % (h, gw), tag=tag)
-            for a in range(4):
-                nc.tensor.transpose(xt[:, a, :], words[:, 512 * gw + 128 * a : 512 * gw + 128 * (a + 1)], ident[:])
-            return xt
-
-        def drain_t(item, xt):
-            h, gw = item
-            i = gw % 4
-            s32 = stages[(h, gw // 4)][:].bitcast(F32)
-            nc.vector.tensor_copy(
-                out=s32[:, 512 * i : 512 * (i + 1)].rearrange("p (g r u) -> p g r u", g=2, r=128, u=2),
-                in_=xt[:].rearrange("p (g u) r -> p g r u", g=2, u=2),
-            )
-
-        def flip(h, j, i0, i1, key, tags):
             if i0 == 0:
-                stages[(h, j)] = stg.tile([P, 4096], BF16, name="stage%d%d" % (h, j), tag="stage%d" % ((4 * h + j) % 3), align_bytes=64)
-            batch(key, tags, [(h, 4 * j + i) for i in range(i0, i1)], fill_t, drain_t)
+                stages[(h, j)] = stg.tile([P, 4096], BF16, name="stage%d%d" % (h, j), tag="stage%d" % ((4 * h + j) % 2), align_bytes=64)
+            s32 = stages[(h, j)][:].bitcast(F32)
+            for i in range(i0, i1):
+                gw = 4 * j + i
+                xt = pst.tile([P, 4, P], F32, name="xt%d_%d" % (h, gw), tag="xt%d" % i)
+                for a in range(4):
+                    nc.tensor.transpose(xt[:, a, :], words[:, 512 * gw + 128 * a : 512 * gw + 128 * (a + 1)], ident[:])
+                dst = s32[:, 512 * i : 512 * (i + 1)].rearrange("p (g r u) -> p g r u", g=2, r=128, u=2)
+                src = xt[:].rearrange("p (g u) r -> p g r u", g=2, u=2)
+                if i == 0:
+                    nc.scalar.copy(out=dst, in_=src)
+                else:
+                    nc.vector.tensor_copy(out=dst, in_=src)
 
         def quant_g(h, j, i0, i1):
             cols = slice(1024 * j + 256 * i0, 1024 * j + 256 * i1)
@@ -118,63 +103,56 @@ def tile_patchpositionembedding_kernel(tc, x, W, b, class_token, pos_emb, grad_o
                 in_=stages[(h, j)][:, 1024 * i0 : 1024 * i1],
             )
 
-        def fill_x(item, tag):
-            h, n, gw = item
-            acc = psum.tile([P, 512], F32, name="acc%d%d_%d" % (h, n, gw), tag=tag)
-            for g in range(2):
-                cols = slice(128 * (2 * gw + g), 128 * (2 * gw + g + 1))
-                nc.tensor.matmul_mx(
-                    out=acc[:],
-                    lhsT=gcodes[h][:, cols].bitcast(E5M2X4),
-                    lhsT_scale=gscales[h][:, cols],
-                    rhs=wcodes[:, g, 512 * n : 512 * (n + 1)].bitcast(E4M3X4),
-                    rhs_scale=wscales[:, g, 512 * n : 512 * (n + 1)],
-                    start=(g == 0),
-                    stop=(g == 1),
-                )
-            return acc
+        otiles = {}
 
-        def drain_x(item, acc):
-            h, n, gw = item
-            nc.scalar.copy(
-                out=otiles[(h, n)][:, :, :, gw, :],
-                in_=acc[:].rearrange("p (c r w) -> p c r w", c=2, r=16, w=16),
-            )
-
-        def mult(h, n, w0, w1, key, tags):
-            if w0 == 0:
+        def mult(h, n, j):
+            if j == 0:
                 otiles[(h, n)] = big.tile([P, 2, 16, 16, 16], F32, name="o%d%d" % (h, n), tag="big%d" % (h if n == 1 else 2 + h))
-            batch(key, tags, [(h, n, gw) for gw in range(w0, w1)], fill_x, drain_x)
-            if w1 == 16:
+            o = otiles[(h, n)]
+            tmp = stg.tile([P, 4, 32, 16], F32, name="tmp%d%d_%d" % (h, n, j), tag="tmp%d" % (j % 2))
+            for i in range(4):
+                gw = 4 * j + i
+                acc = psa.tile([P, 512], F32, name="acc%d%d_%d" % (h, n, gw), tag="acc%d" % i)
+                for g in range(2):
+                    cols = slice(128 * (2 * gw + g), 128 * (2 * gw + g + 1))
+                    nc.tensor.matmul_mx(
+                        out=acc[:],
+                        lhsT=gcodes[h][:, cols].bitcast(E5M2X4),
+                        lhsT_scale=gscales[h][:, cols],
+                        rhs=wcodes[:, g, 512 * n : 512 * (n + 1)].bitcast(E4M3X4),
+                        rhs_scale=wscales[:, g, 512 * n : 512 * (n + 1)],
+                        start=(g == 0),
+                        stop=(g == 1),
+                    )
+                nc.scalar.copy(out=tmp[:, i], in_=acc[:].rearrange("p (a x) -> p a x", x=16))
+            nc.vector.tensor_copy(
+                out=o[:, :, :, 4 * j : 4 * j + 4, :].rearrange("p c r i x -> p (c r) i x"),
+                in_=tmp[:].rearrange("p i a x -> p a i x"),
+            )
+            if j == 3:
                 for c in range(2):
                     nc.sync.dma_start(
                         out=out[:, 2 * n + c, 128 * h : 128 * (h + 1), :].rearrange("b (g r) x -> b g (r x)", g=8),
-                        in_=otiles[(h, n)][:, c].rearrange("p r w x -> p (r w x)"),
+                        in_=o[:, c].rearrange("p r w x -> p (r w x)"),
                     )
 
-        LOW = ["pb0", "pb1", "pb2", "pb3"]
-        HIGH = ["pb4", "pb5", "pb6", "pb7"]
-
-        flip(0, 0, 0, 2, "ta", LOW[0:2])
+        flip(0, 0, 0, 2)
         regroup_w(0, 0)
         quant_g(0, 0, 0, 2)
         regroup_w(0, 1)
         quant_w(0, 0)
         quant_w(0, 1)
-        flip(0, 0, 2, 4, "tb", LOW[2:4])
+        flip(0, 0, 2, 4)
         quant_g(0, 0, 2, 4)
         quads = [(h, j) for h in range(2) for j in range(4)]
         late_w = [lambda: regroup_w(1, 0), lambda: quant_w(1, 0), lambda: regroup_w(1, 1), lambda: quant_w(1, 1)]
         for t in range(8):
             if t + 1 < 8:
                 h, j = quads[t + 1]
-                flip(h, j, 0, 4, "t", LOW)
+                flip(h, j, 0, 4)
                 quant_g(h, j, 0, 4)
             if t >= 4:
                 late_w[t - 4]()
-            h, j = quads[t]
-            mult(h, 0, 4 * j, 4 * j + 2, "xa", HIGH[0:2])
-            mult(h, 0, 4 * j + 2, 4 * j + 4, "xb", HIGH[2:4])
-        for t in range(8):
-            h, j = quads[t]
-            mult(h, 1, 4 * j, 4 * j + 4, "m%d" % (t % 2), LOW if t % 2 == 0 else HIGH)
+            mult(quads[t][0], 0, quads[t][1])
+        for h, j in quads:
+            mult(h, 1, j)

@@ -29,35 +29,29 @@ def tile_patchpositionembedding_kernel(tc, x, W, b, class_token, pos_emb, grad_o
         make_identity(nc, ident[:])
         ctx.enter_context(tc.manual_schedule())
 
-        wraw = [keep.tile([P, 8, 512], BF16, name="wraw%d" % n) for n in range(2)]
+        wraw = keep.tile([P, 8, 1024], BF16, name="wraw")
         wcodes = keep.tile([P, 2, 1024], U32, name="wcodes", align_bytes=64)
         wscales = keep.tile([P, 2, 1024], U8, name="wscales", align_bytes=64)
         gcodes = [keep.tile([P, 4096], U32, name="gcodes%d" % h, align_bytes=64) for h in range(2)]
         gscales = [keep.tile([P, 4096], U8, name="gscales%d" % h, align_bytes=64) for h in range(2)]
         graw = [big.tile([P, 16 * 1024], BF16, name="graw%d" % h, tag="big%d" % h) for h in range(2)]
 
-        def load_g(h, w0, w1):
+        def load_g(queue, h, w0, w1):
             src = grad_out[:, 1 + 128 * h : 1 + 128 * (h + 1), :].rearrange("b (g w) k -> b g w k", g=8)
-            nc.sync.dma_start(
+            queue.dma_start(
                 out=graw[h][:, w0 * 1024 : w1 * 1024],
                 in_=src[:, :, w0:w1, :].rearrange("b g w k -> b g (w k)"),
             )
 
-        def load_w(n):
-            for a in range(4):
-                nc.sync.dma_start(
-                    out=wraw[n][:, 2 * a : 2 * a + 2, :],
-                    in_=W[256 * a : 256 * (a + 1), 512 * n : 512 * (n + 1)].rearrange("(q e) c -> q e c", e=2),
-                )
-
-        load_g(0, 0, 2)
-        load_w(0)
-        load_g(0, 2, 4)
-        for j in range(1, 4):
-            load_g(0, 4 * j, 4 * j + 4)
-        for j in range(4):
-            load_g(1, 4 * j, 4 * j + 4)
-        load_w(1)
+        nc.sync.dma_start(
+            out=wraw[:].rearrange("p (a e) n -> p a (e n)", e=2),
+            in_=W.rearrange("(a q e) n -> q a (e n)", a=4, q=128, e=2),
+        )
+        for h in range(2):
+            load_g(nc.gpsimd, h, 0, 4)
+            load_g(nc.sync, h, 4, 8)
+            load_g(nc.gpsimd, h, 8, 12)
+            load_g(nc.sync, h, 12, 16)
 
         wgs = {}
 
@@ -66,7 +60,7 @@ def tile_patchpositionembedding_kernel(tc, x, W, b, class_token, pos_emb, grad_o
             wgs[(n, g)] = wg
             nc.vector.tensor_copy(
                 out=wg[:].rearrange("p (c i) t -> p c t i", i=4),
-                in_=wraw[n][:, 4 * g : 4 * g + 4, :].rearrange("p t (c i) -> p c t i", i=4),
+                in_=wraw[:, 4 * g : 4 * g + 4, 512 * n : 512 * (n + 1)].rearrange("p t (c i) -> p c t i", i=4),
             )
 
         def quant_w(n, g):
@@ -81,7 +75,7 @@ def tile_patchpositionembedding_kernel(tc, x, W, b, class_token, pos_emb, grad_o
         def flip(h, j, i0, i1):
             words = graw[h][:].bitcast(F32)
             if i0 == 0:
-                stages[(h, j)] = stg.tile([P, 4096], BF16, name="stage%d%d" % (h, j), tag="stage%d" % ((4 * h + j) % 2), align_bytes=64)
+                stages[(h, j)] = stg.tile([P, 4096], BF16, name="stage%d%d" % (h, j), tag="stage%d" % ((4 * h + j) % 3), align_bytes=64)
             s32 = stages[(h, j)][:].bitcast(F32)
             for i in range(i0, i1):
                 gw = 4 * j + i
@@ -109,7 +103,6 @@ def tile_patchpositionembedding_kernel(tc, x, W, b, class_token, pos_emb, grad_o
             if j == 0:
                 otiles[(h, n)] = big.tile([P, 2, 16, 16, 16], F32, name="o%d%d" % (h, n), tag="big%d" % (h if n == 1 else 2 + h))
             o = otiles[(h, n)]
-            tmp = stg.tile([P, 4, 32, 16], F32, name="tmp%d%d_%d" % (h, n, j), tag="tmp%d" % (j % 2))
             for i in range(4):
                 gw = 4 * j + i
                 acc = psa.tile([P, 512], F32, name="acc%d%d_%d" % (h, n, gw), tag="acc%d" % i)
@@ -124,14 +117,11 @@ def tile_patchpositionembedding_kernel(tc, x, W, b, class_token, pos_emb, grad_o
                         start=(g == 0),
                         stop=(g == 1),
                     )
-                nc.scalar.copy(out=tmp[:, i], in_=acc[:].rearrange("p (a x) -> p a x", x=16))
-            nc.vector.tensor_copy(
-                out=o[:, :, :, 4 * j : 4 * j + 4, :].rearrange("p c r i x -> p (c r) i x"),
-                in_=tmp[:].rearrange("p i a x -> p a i x"),
-            )
+                src = acc[:].rearrange("p (c r w) -> p c r w", c=2, r=16, w=16)
+                nc.scalar.copy(out=o[:, :, :, gw, :], in_=src)
             if j == 3:
                 for c in range(2):
-                    nc.sync.dma_start(
+                    (nc.sync if c == 0 else nc.gpsimd).dma_start(
                         out=out[:, 2 * n + c, 128 * h : 128 * (h + 1), :].rearrange("b (g r) x -> b g (r x)", g=8),
                         in_=o[:, c].rearrange("p r w x -> p (r w x)"),
                     )

from contextlib import ExitStack

import concourse.mybir as mybir
from concourse.masks import make_identity

F32 = mybir.dt.float32
BF16 = mybir.dt.bfloat16
U32 = mybir.dt.uint32
U8 = mybir.dt.uint8
E4M3X4 = mybir.dt.float8_e4m3fn_x4
E5M2X4 = mybir.dt.float8_e5m2_x4

P = 128
FLOPS = 2 * 4096 * 1024 * 1024
BYTES = 4096 * 1024 * 2 + 1024 * 1024 * 2 + 4096 * 1024 * 4


def tile_patchpositionembedding_kernel(tc, x, W, b, class_token, pos_emb, grad_out, out):
    nc = tc.nc
    with ExitStack() as ctx:
        keep = ctx.enter_context(tc.tile_pool(name="keep", bufs=1))
        big = ctx.enter_context(tc.tile_pool(name="big", bufs=1))
        stg = ctx.enter_context(tc.tile_pool(name="stg", bufs=1))
        wst = ctx.enter_context(tc.tile_pool(name="wst", bufs=1))
        pst = ctx.enter_context(tc.psum_pool(name="pst", bufs=1))
        psa = ctx.enter_context(tc.psum_pool(name="psa", bufs=1))

        ident = keep.tile([P, P], F32, name="ident")
        make_identity(nc, ident[:])
        ctx.enter_context(tc.manual_schedule())

        wraw = keep.tile([P, 8, 1024], BF16, name="wraw")
        wcodes = keep.tile([P, 2, 1024], U32, name="wcodes", align_bytes=64)
        wscales = keep.tile([P, 2, 1024], U8, name="wscales", align_bytes=64)
        gcodes = [keep.tile([P, 4096], U32, name="gcodes%d" % h, align_bytes=64) for h in range(2)]
        gscales = [keep.tile([P, 4096], U8, name="gscales%d" % h, align_bytes=64) for h in range(2)]
        graw = [big.tile([P, 16 * 1024], BF16, name="graw%d" % h, tag="big%d" % h) for h in range(2)]

        def load_g(queue, h, w0, w1):
            src = grad_out[:, 1 + 128 * h : 1 + 128 * (h + 1), :].rearrange("b (g w) k -> b g w k", g=8)
            queue.dma_start(
                out=graw[h][:, w0 * 1024 : w1 * 1024],
                in_=src[:, :, w0:w1, :].rearrange("b g w k -> b g (w k)"),
            )

        nc.sync.dma_start(
            out=wraw[:].rearrange("p (a e) n -> p a (e n)", e=2),
            in_=W.rearrange("(a q e) n -> q a (e n)", a=4, q=128, e=2),
        )
        for h in range(2):
            load_g(nc.gpsimd, h, 0, 4)
            load_g(nc.sync, h, 4, 8)
            load_g(nc.gpsimd, h, 8, 12)
            load_g(nc.sync, h, 12, 16)

        wgs = {}

        def regroup_w(n, g):
            wg = wst.tile([P, 512, 4], BF16, name="wg%d%d" % (n, g), tag="wg%d" % g, align_bytes=64)
            wgs[(n, g)] = wg
            nc.vector.tensor_copy(
                out=wg[:].rearrange("p (c i) t -> p c t i", i=4),
                in_=wraw[:, 4 * g : 4 * g + 4, 512 * n : 512 * (n + 1)].rearrange("p t (c i) -> p c t i", i=4),
            )

        def quant_w(n, g):
            nc.vector.quantize_mx(
                out=wcodes[:, g, 512 * n : 512 * (n + 1)].bitcast(E4M3X4),
                scales=wscales[:, g, 512 * n : 512 * (n + 1)],
                in_=wgs[(n, g)][:].rearrange("p c t -> p (c t)"),
            )

        stages = {}

        def flip(h, j, i0, i1):
            words = graw[h][:].bitcast(F32)
            if i0 == 0:
                stages[(h, j)] = stg.tile([P, 4096], BF16, name="stage%d%d" % (h, j), tag="stage%d" % ((4 * h + j) % 3), align_bytes=64)
            s32 = stages[(h, j)][:].bitcast(F32)
            for i in range(i0, i1):
                gw = 4 * j + i
                xt = pst.tile([P, 4, P], F32, name="xt%d_%d" % (h, gw), tag="xt%d" % i)
                for a in range(4):
                    nc.tensor.transpose(xt[:, a, :], words[:, 512 * gw + 128 * a : 512 * gw + 128 * (a + 1)], ident[:])
                dst = s32[:, 512 * i : 512 * (i + 1)].rearrange("p (g r u) -> p g r u", g=2, r=128, u=2)
                src = xt[:].rearrange("p (g u) r -> p g r u", g=2, u=2)
                if i == 0:
                    nc.scalar.copy(out=dst, in_=src)
                else:
                    nc.vector.tensor_copy(out=dst, in_=src)

        def quant_g(h, j, i0, i1):
            cols = slice(1024 * j + 256 * i0, 1024 * j + 256 * i1)
            nc.vector.quantize_mx(
                out=gcodes[h][:, cols].bitcast(E5M2X4),
                scales=gscales[h][:, cols],
                in_=stages[(h, j)][:, 1024 * i0 : 1024 * i1],
            )

        otiles = {}

        def mult(h, n, j):
            if j == 0:
                otiles[(h, n)] = big.tile([P, 2, 16, 16, 16], F32, name="o%d%d" % (h, n), tag="big%d" % (h if n == 1 else 2 + h))
            o = otiles[(h, n)]
            for i in range(4):
                gw = 4 * j + i
                acc = psa.tile([P, 512], F32, name="acc%d%d_%d" % (h, n, gw), tag="acc%d" % i)
                for g in range(2):
                    cols = slice(128 * (2 * gw + g), 128 * (2 * gw + g + 1))
                    nc.tensor.matmul_mx(
                        out=acc[:],
                        lhsT=gcodes[h][:, cols].bitcast(E5M2X4),
                        lhsT_scale=gscales[h][:, cols],
                        rhs=wcodes[:, g, 512 * n : 512 * (n + 1)].bitcast(E4M3X4),
                        rhs_scale=wscales[:, g, 512 * n : 512 * (n + 1)],
                        start=(g == 0),
                        stop=(g == 1),
                    )
                src = acc[:].rearrange("p (c r w) -> p c r w", c=2, r=16, w=16)
                nc.scalar.copy(out=o[:, :, :, gw, :], in_=src)
            if j == 3:
                for c in range(2):
                    (nc.sync if c == 0 else nc.gpsimd).dma_start(
                        out=out[:, 2 * n + c, 128 * h : 128 * (h + 1), :].rearrange("b (g r) x -> b g (r x)", g=8),
                        in_=o[:, c].rearrange("p r w x -> p (r w x)"),
                    )

        flip(0, 0, 0, 2)
        regroup_w(0, 0)
        quant_g(0, 0, 0, 2)
        regroup_w(0, 1)
        quant_w(0, 0)
        quant_w(0, 1)
        flip(0, 0, 2, 4)
        quant_g(0, 0, 2, 4)
        quads = [(h, j) for h in range(2) for j in range(4)]
        late_w = [lambda: regroup_w(1, 0), lambda: quant_w(1, 0), lambda: regroup_w(1, 1), lambda: quant_w(1, 1)]
        for t in range(8):
            if t + 1 < 8:
                h, j = quads[t + 1]
                flip(h, j, 0, 4)
                quant_g(h, j, 0, 4)
            if t >= 4:
                late_w[t - 4]()
            mult(quads[t][0], 0, quads[t][1])
        for h, j in quads:
            mult(h, 1, j)
